import numpy as np
import ml_dtypes


def mxq(x, axis, fmt="e4m3"):
    dtype, down = {"e4m3": (ml_dtypes.float8_e4m3fn, 7), "e5m2": (ml_dtypes.float8_e5m2, 14)}[fmt]
    v = np.moveaxis(np.asarray(x, np.float32).astype(ml_dtypes.bfloat16).astype(np.float64), axis, -1)
    blocks = v.reshape(v.shape[:-1] + (-1, 32))
    amax = np.abs(blocks).max(-1, keepdims=True)
    byte = np.maximum(np.where(amax > 0, np.frexp(amax)[1] - 1 + 127, 0) - down, 1)
    scale = np.exp2(byte - 127.0)
    codes = (blocks / scale).astype(np.float32).astype(dtype).astype(np.float64)
    return np.moveaxis((codes * scale).reshape(v.shape), -1, axis)


WIDE = False


def mx_kscale(k):
    if not WIDE:
        return np.ones(k)
    levels = np.array([10, -10, 5, -5, 0])
    if k % 512:
        return np.exp2(np.random.permutation(np.resize(levels, k // 32))).repeat(32)
    a = np.empty((k // 512, 16))
    for p in range(k // 512):
        a[p, :8] = np.random.permutation(np.resize(levels, 8))
        for g in range(8):
            far = levels[np.abs(levels - a[p, g]) >= 10]
            a[p, g + 8] = far[np.random.randint(len(far))]
    return np.exp2(a.ravel()).repeat(32)


BF16 = ml_dtypes.bfloat16


def bf(x):
    return np.asarray(x, np.float32).astype(BF16)


def f64(x):
    return np.asarray(x).astype(np.float64)


B, C, T, DK, DV, P = 1, 1024, 2048, 128, 512, 4


def maxpool(y):
    b, ch, t = y.shape
    return y.reshape(b, ch, t // P, P).max(axis=-1)


def draw0():
    s = mx_kscale(C)
    return {"x": bf(np.random.standard_normal((B, C, T)) * s[:, None]),
            "Wq": bf(np.random.standard_normal((DK, C)) * 0.5 / np.sqrt(C) / s),
            "Wk": bf(np.random.standard_normal((DK, C)) * 0.5 / np.sqrt(C) / s),
            "Wv": bf(np.random.standard_normal((DV, C)) / np.sqrt(C) / s)}


def core(x, Wq, Wk, Wv):
    xq = mxq(f64(x), 1, "e4m3")
    q = mxq(f64(Wq), 1, "e4m3") @ xq
    k = maxpool(mxq(f64(Wk), 1, "e4m3") @ xq)
    v = maxpool(mxq(f64(Wv), 1, "e4m3") @ xq)
    return q, k, v


def e4m3fn_bytes(y):
    return np.clip(np.asarray(y, np.float64), -448.0, 448.0).astype(np.float32).astype(ml_dtypes.float8_e4m3fn).view(np.uint8)


def e4m3fn_values(b):
    return np.asarray(b, np.uint8).view(ml_dtypes.float8_e4m3fn).astype(np.float64)


def setup_inputs():
    d = draw0()
    x0 = np.asarray(d['x']).astype(np.float64)
    s = (np.max(np.abs(x0), axis=(0, 2), keepdims=True) / 448.0).astype(np.float32)
    out = {}
    for k, v in d.items():
        if k == 'x':
            out['x_bytes'] = e4m3fn_bytes(x0 / s.astype(np.float64))
            out['x_scale'] = s
        else:
            out[k] = v
    return out


def reference(x_bytes, x_scale, Wq, Wk, Wv):
    return core(e4m3fn_values(x_bytes) * x_scale.astype(np.float64), Wq, Wk, Wv)

@@ -1,0 +1,239 @@
+from contextlib import ExitStack
+
+import concourse.mybir as mybir
+from concourse.masks import make_identity
+
+FLOPS = 2 * 768 * 1024 * 2048
+
+F32 = mybir.dt.float32
+BF16 = mybir.dt.bfloat16
+U32 = mybir.dt.uint32
+U8 = mybir.dt.uint8
+FP8 = mybir.dt.float8_e4m3fn
+FP8X4 = mybir.dt.float8_e4m3fn_x4
+ACT = mybir.ActivationFunctionType
+ALU = mybir.AluOpType
+AX = mybir.AxisListType
+
+P = 128
+PACK = 4
+PASSES = 2
+T_ALL = 2048
+CH = 512
+NCH = T_ALL // CH
+HALF = CH // 2
+WIN = 4
+MT = 6
+G_G, G_V = 1, 0
+
+WIDEN = (("SSVV", "SSVV"), ("SSVV", "SSSS"), ("SSVV", "SSSS"), ("SSVV", "SSSS"))
+INTER = (("VV", "SV"), ("SV", "GG"), ("SV", "GG"), ("SV", "GG"))
+
+
+def tile_selfattention_pa_kernel(tc, x_bytes, x_scale, Wq, Wk, Wv, out_0, out_1, out_2):
+    nc = tc.nc
+    x_rows = x_bytes.flatten_outer_dims().rearrange("(g p t) n -> g p t n", p=P, t=PACK)
+    s_rows = x_scale.flatten_outer_dims().rearrange("(g p t) o -> p g (t o)", p=P, t=PACK)
+    wv_rows = Wv.rearrange("(m p) k -> m p k", p=P)
+    w_src = [Wq, Wk] + [wv_rows[i] for i in range(4)]
+    q_out = out_0.flatten_outer_dims()
+    k_out = out_1.flatten_outer_dims()
+    v_out = out_2.flatten_outer_dims().rearrange("(m p) w -> p m w", p=P)
+
+    with ExitStack() as ctx:
+        keep = ctx.enter_context(tc.tile_pool(name="keep", bufs=1))
+        psum = ctx.enter_context(tc.psum_pool(name="psum", bufs=8))
+
+        ident = keep.tile([P, P], F32, name="ident")
+        make_identity(nc, ident[:])
+        warm = keep.tile([P, 2], F32, name="warm")
+        nc.vector.memset(warm[:], 0.0)
+
+        scale = keep.tile([P, PASSES, PACK], F32, name="scale")
+        xb = {}
+        wide = {}
+        xc = {}
+        xs = {}
+        for c in range(NCH):
+            for g in range(PASSES):
+                xb[c, g] = keep.tile([P, PACK, CH], U8, name="xbytes%d%d" % (c, g))
+                wide[c, g] = keep.tile([P, PACK, CH], BF16, name="wide%d%d" % (c, g))
+                xc[c, g] = keep.tile([P, CH], U32, name="xcodes%d%d" % (c, g), align_bytes=64)
+                xs[c, g] = keep.tile([P, CH], U8, name="xscales%d%d" % (c, g), align_bytes=64)
+        w_raw = [keep.tile([P, PASSES * 512], BF16, name="wraw%d" % m) for m in range(MT)]
+        w_grp = [keep.tile([P, PASSES * 512], BF16, name="wgrp%d" % m, align_bytes=64) for m in range(MT)]
+        w_cod = [keep.tile([P, PASSES * P], U32, name="wcodes%d" % m, align_bytes=64) for m in range(MT)]
+        w_scl = [keep.tile([P, PASSES * P], U8, name="wscales%d" % m, align_bytes=64) for m in range(MT)]
+        q_sb = [keep.tile([P, CH], F32, name="qsb%d" % c) for c in range(NCH)]
+        kv_sb = [keep.tile([P, MT - 1, CH // WIN], F32, name="kvsb%d" % c) for c in range(NCH)]
+        grp = {}
+        w_ps = {}
+        acc = {}
+
+        def load_x(c, g):
+            nc.sync.dma_start(out=xb[c, g][:], in_=x_rows[g][:, :, c * CH:(c + 1) * CH])
+
+        def load_w(m):
+            nc.sync.dma_start(out=w_raw[m][:], in_=w_src[m])
+
+        def widen(c, g, who):
+            for t in range(PACK):
+                if WIDEN[c][g][t] != who:
+                    continue
+                src = xb[c, g][:, t, :].bitcast(FP8)
+                dst = wide[c, g][:, t, :]
+                col = scale[:, g, t:t + 1]
+                if who == "S":
+                    nc.scalar.activation(out=dst, in_=src, func=ACT.Copy, scale=col)
+                else:
+                    nc.vector.tensor_scalar(out=dst, in0=src, scalar1=col, scalar2=None, op0=ALU.mult)
+
+        def inter(c, g, who):
+            for h in range(2):
+                if INTER[c][g][h] != who:
+                    continue
+                if (c, g) not in grp:
+                    if g == G_G:
+                        grp[c, g] = keep.tile([P, CH, PACK], BF16, name="grpg%d" % c, tag="grpg", bufs=1, align_bytes=64)
+                    else:
+                        grp[c, g] = keep.tile([P, CH, PACK], BF16, name="grpv%d" % c, tag="grpv", bufs=2, align_bytes=64)
+                cols = slice(h * HALF, (h + 1) * HALF)
+                dst = grp[c, g][:, cols, :]
+                src = wide[c, g][:, :, cols].rearrange("p t n -> p n t")
+                if who == "V":
+                    nc.vector.tensor_copy(out=dst, in_=src)
+                elif who == "S":
+                    nc.scalar.copy(out=dst, in_=src)
+                else:
+                    nc.gpsimd.tensor_scalar(out=dst, in0=src, scalar1=1.0, scalar2=0.0, op0=ALU.mult, op1=ALU.add)
+
+        def quant(c, g):
+            nc.vector.quantize_mx(
+                out=xc[c, g][:].bitcast(FP8X4),
+                scales=xs[c, g][:],
+                in_=grp[c, g][:].rearrange("p n t -> p (n t)"),
+            )
+
+        def w_turn(m):
+            w_ps[m] = psum.tile([P, PASSES, 2, P], F32, name="wps%d" % m, tag="bank")
+            words = w_raw[m][:].bitcast(F32)
+            for g in range(PASSES):
+                for u in range(2):
+                    nc.tensor.transpose(w_ps[m][:, g, u, :], words[:, 256 * g + u:256 * (g + 1):2], ident[:])
+
+        def w_out(m, who):
+            dst = w_grp[m][:].bitcast(F32).rearrange("p (g r u) -> p g r u", g=PASSES, u=2)
+            src = w_ps[m][:].rearrange("p g u r -> p g r u")
+            if who == "V":
+                nc.vector.tensor_copy(out=dst, in_=src)
+            else:
+                nc.scalar.copy(out=dst, in_=src)
+
+        def w_quant(m):
+            nc.vector.quantize_mx(out=w_cod[m][:].bitcast(FP8X4), scales=w_scl[m][:], in_=w_grp[m][:])
+
+        def mult(c, m):
+            acc[c, m] = psum.tile([P, CH], F32, name="acc%d%d" % (c, m), tag="bank")
+            for g in range(PASSES):
+                rows = slice(g * P, (g + 1) * P)
+                nc.tensor.matmul_mx(
+                    out=acc[c, m][:],
+                    lhsT=w_cod[m][:, rows].bitcast(FP8X4),
+                    lhsT_scale=w_scl[m][:, rows],
+                    rhs=xc[c, g][:].bitcast(FP8X4),
+                    rhs_scale=xs[c, g][:],
+                    start=(g == 0),
+                    stop=(g == PASSES - 1),
+                )
+
+        def pool(c, m):
+            nc.vector.tensor_reduce(
+                out=kv_sb[c][:, m - 1, :],
+                in_=acc[c, m][:].rearrange("p (w j) -> p w j", j=WIN),
+                axis=AX.X,
+                op=ALU.max,
+            )
+
+        def store_kv(c):
+            cols = slice(c * (CH // WIN), (c + 1) * (CH // WIN))
+            nc.sync.dma_start(out=k_out[:, cols], in_=kv_sb[c][:, 0, :])
+            nc.sync.dma_start(out=v_out[:, :, cols], in_=kv_sb[c][:, 1:MT - 1, :])
+
+        def q_copy(c):
+            nc.scalar.copy(out=q_sb[c][:], in_=acc[c, 0][:])
+            nc.sync.dma_start(out=q_out[:, c * CH:(c + 1) * CH], in_=q_sb[c][:])
+
+        with tc.manual_schedule():
+            nc.sync.dma_start(out=scale[:], in_=s_rows)
+            load_x(0, 0)
+            load_x(0, 1)
+            for m in (0, 1, 2):
+                load_w(m)
+            load_x(1, G_G)
+            load_x(1, G_V)
+            for m in (3, 4, 5):
+                load_w(m)
+            for c in (2, 3):
+                load_x(c, G_G)
+                load_x(c, G_V)
+            nc.scalar.activation(out=warm[:, 1:2], in_=warm[:, 0:1], func=ACT.Copy, scale=1.0)
+
+            for g in range(PASSES):
+                widen(0, g, "S")
+                widen(0, g, "V")
+            inter(0, 0, "V")
+            inter(0, 0, "S")
+            quant(0, 0)
+            inter(0, 1, "S")
+            inter(0, 1, "V")
+            for m in (0, 1, 2):
+                w_turn(m)
+            w_out(0, "V")
+            w_out(1, "V")
+            w_out(2, "S")
+            quant(0, 1)
+            for m in (0, 1, 2):
+                w_quant(m)
+            widen(1, G_G, "S")
+            widen(1, G_G, "V")
+            inter(1, G_G, "G")
+            widen(1, G_V, "V")
+            for m in (3, 4, 5):
+                w_turn(m)
+                w_out(m, "S")
+            for m in (1, 2):
+                mult(0, m)
+                pool(0, m)
+            for m in (3, 4, 5):
+                w_quant(m)
+            for m in (3, 4, 5):
+                mult(0, m)
+                pool(0, m)
+            mult(0, 0)
+            store_kv(0)
+            widen(1, G_V, "S")
+            inter(1, G_G, "S")
+            inter(1, G_V, "S")
+            widen(2, G_G, "S")
+
+            for s in range(1, NCH):
+                inter(s, G_G, "V")
+                inter(s, G_V, "V")
+                quant(s, G_G)
+                quant(s, G_V)
+                if s + 1 < NCH:
+                    widen(s + 1, G_G, "V")
+                    widen(s + 1, G_V, "V")
+                    inter(s + 1, G_G, "G")
+                    widen(s + 1, G_V, "S")
+                    inter(s + 1, G_G, "S")
+                    inter(s + 1, G_V, "S")
+                q_copy(s - 1)
+                if s + 2 < NCH:
+                    widen(s + 2, G_G, "S")
+                for m in (1, 2, 3, 4, 5):
+                    mult(s, m)
+                    pool(s, m)
+                mult(s, 0)
+                store_kv(s)
+            q_copy(NCH - 1)

@@ -24,10 +24,10 @@ NCH = T_ALL // CH
 HALF = CH // 2
 WIN = 4
 MT = 6
-G_G, G_V = 1, 0
+M_ORDER = (1, 2, 3, 4, 5, 0)
 
-WIDEN = (("SSVV", "SSVV"), ("SSVV", "SSSS"), ("SSVV", "SSSS"), ("SSVV", "SSSS"))
-INTER = (("VV", "SV"), ("SV", "GG"), ("SV", "GG"), ("SV", "GG"))
+WIDEN = (("SVVV", "SSVV"), ("SSVV", "SSVV"), ("SSVV", "SSVV"), ("SSSS", "SSVV"))
+INTER = (("VT", "VT"), ("TT", "GG"), ("TT", "GG"), ("TT", "GG"))
 
 
 def tile_selfattention_pa_kernel(tc, x_bytes, x_scale, Wq, Wk, Wv, out_0, out_1, out_2):
@@ -46,29 +46,30 @@ def tile_selfattention_pa_kernel(tc, x_bytes, x_scale, Wq, Wk, Wv, out_0, out_1,
 
         ident = keep.tile([P, P], F32, name="ident")
         make_identity(nc, ident[:])
+        ident_bf = keep.tile([P, P], BF16, name="identbf")
+        make_identity(nc, ident_bf[:])
         warm = keep.tile([P, 2], F32, name="warm")
         nc.vector.memset(warm[:], 0.0)
 
         scale = keep.tile([P, PASSES, PACK], F32, name="scale")
         xb = {}
         wide = {}
-        xc = {}
-        xs = {}
         for c in range(NCH):
             for g in range(PASSES):
                 xb[c, g] = keep.tile([P, PACK, CH], U8, name="xbytes%d%d" % (c, g))
                 wide[c, g] = keep.tile([P, PACK, CH], BF16, name="wide%d%d" % (c, g))
-                xc[c, g] = keep.tile([P, CH], U32, name="xcodes%d%d" % (c, g), align_bytes=64)
-                xs[c, g] = keep.tile([P, CH], U8, name="xscales%d%d" % (c, g), align_bytes=64)
+        grp = [keep.tile([P, PASSES, CH, PACK], BF16, name="grp%d" % c, align_bytes=64) for c in range(NCH)]
+        xc = [keep.tile([P, PASSES, CH], U32, name="xcodes%d" % c, align_bytes=64) for c in range(NCH)]
+        xs = [keep.tile([P, PASSES, CH], U8, name="xscales%d" % c, align_bytes=64) for c in range(NCH)]
         w_raw = [keep.tile([P, PASSES * 512], BF16, name="wraw%d" % m) for m in range(MT)]
-        w_grp = [keep.tile([P, PASSES * 512], BF16, name="wgrp%d" % m, align_bytes=64) for m in range(MT)]
-        w_cod = [keep.tile([P, PASSES * P], U32, name="wcodes%d" % m, align_bytes=64) for m in range(MT)]
-        w_scl = [keep.tile([P, PASSES * P], U8, name="wscales%d" % m, align_bytes=64) for m in range(MT)]
+        w_grp = keep.tile([P, MT, PASSES * 512], BF16, name="wgrp", align_bytes=64)
+        w_cod = keep.tile([P, MT, PASSES * P], U32, name="wcodes", align_bytes=64)
+        w_scl = keep.tile([P, MT, PASSES * P], U8, name="wscales", align_bytes=64)
         q_sb = [keep.tile([P, CH], F32, name="qsb%d" % c) for c in range(NCH)]
         kv_sb = [keep.tile([P, MT - 1, CH // WIN], F32, name="kvsb%d" % c) for c in range(NCH)]
-        grp = {}
         w_ps = {}
         acc = {}
+        il_ps = {}
 
         def load_x(c, g):
             nc.sync.dma_start(out=xb[c, g][:], in_=x_rows[g][:, :, c * CH:(c + 1) * CH])
@@ -78,78 +79,95 @@ def tile_selfattention_pa_kernel(tc, x_bytes, x_scale, Wq, Wk, Wv, out_0, out_1,
 
         def widen(c, g, who):
             for t in range(PACK):
-                if WIDEN[c][g][t] != who:
-                    continue
-                src = xb[c, g][:, t, :].bitcast(FP8)
-                dst = wide[c, g][:, t, :]
-                col = scale[:, g, t:t + 1]
-                if who == "S":
-                    nc.scalar.activation(out=dst, in_=src, func=ACT.Copy, scale=col)
-                else:
-                    nc.vector.tensor_scalar(out=dst, in0=src, scalar1=col, scalar2=None, op0=ALU.mult)
+                if WIDEN[c][g][t] == who:
+                    src = xb[c, g][:, t, :].bitcast(FP8)
+                    dst = wide[c, g][:, t, :]
+                    col = scale[:, g, t:t + 1]
+                    if who == "S":
+                        nc.scalar.activation(out=dst, in_=src, func=ACT.Copy, scale=col)
+                    else:
+                        nc.vector.tensor_scalar(out=dst, in0=src, scalar1=col, scalar2=None, op0=ALU.mult)
 
         def inter(c, g, who):
             for h in range(2):
-                if INTER[c][g][h] != who:
-                    continue
-                if (c, g) not in grp:
-                    if g == G_G:
-                        grp[c, g] = keep.tile([P, CH, PACK], BF16, name="grpg%d" % c, tag="grpg", bufs=1, align_bytes=64)
+                if INTER[c][g][h] == who:
+                    cols = slice(h * HALF, (h + 1) * HALF)
+                    dst = grp[c][:, g, cols, :]
+                    src = wide[c, g][:, :, cols].rearrange("p t n -> p n t")
+                    if who == "V":
+                        nc.vector.tensor_copy(out=dst, in_=src)
+                    elif who == "S":
+                        nc.scalar.copy(out=dst, in_=src)
+                    elif who == "G":
+                        nc.gpsimd.tensor_scalar(out=dst, in0=src, scalar1=1.0, scalar2=0.0, op0=ALU.mult, op1=ALU.add)
                     else:
-                        grp[c, g] = keep.tile([P, CH, PACK], BF16, name="grpv%d" % c, tag="grpv", bufs=2, align_bytes=64)
-                cols = slice(h * HALF, (h + 1) * HALF)
-                dst = grp[c, g][:, cols, :]
-                src = wide[c, g][:, :, cols].rearrange("p t n -> p n t")
-                if who == "V":
-                    nc.vector.tensor_copy(out=dst, in_=src)
-                elif who == "S":
-                    nc.scalar.copy(out=dst, in_=src)
-                else:
-                    nc.gpsimd.tensor_scalar(out=dst, in0=src, scalar1=1.0, scalar2=0.0, op0=ALU.mult, op1=ALU.add)
+                        il_ps[c, g, h] = psum.tile([P, HALF, PACK], BF16, name="ilps%d%d%d" % (c, g, h), tag="bank")
+                        for j in range(2):
+                            part = slice(j * P, (j + 1) * P)
+                            nc.tensor.matmul(
+                                out=il_ps[c, g, h][:, part, :],
+                                lhsT=ident_bf[:],
+                                rhs=src[:, part, :],
+                                start=True,
+                                stop=True,
+                            )
 
-        def quant(c, g):
+        def inter_out(c, g, who):
+            for h in range(2):
+                if INTER[c][g][h] == "T":
+                    cols = slice(h * HALF, (h + 1) * HALF)
+                    if who == "S":
+                        nc.scalar.copy(out=grp[c][:, g, cols, :], in_=il_ps[c, g, h][:])
+                    else:
+                        nc.vector.tensor_copy(out=grp[c][:, g, cols, :], in_=il_ps[c, g, h][:])
+
+        def quant(c):
             nc.vector.quantize_mx(
-                out=xc[c, g][:].bitcast(FP8X4),
-                scales=xs[c, g][:],
-                in_=grp[c, g][:].rearrange("p n t -> p (n t)"),
+                out=xc[c][:].rearrange("p g n -> p (g n)").bitcast(FP8X4),
+                scales=xs[c][:].rearrange("p g n -> p (g n)"),
+                in_=grp[c][:].rearrange("p g n t -> p (g n t)"),
             )
 
-        def w_turn(m):
-            w_ps[m] = psum.tile([P, PASSES, 2, P], F32, name="wps%d" % m, tag="bank")
-            words = w_raw[m][:].bitcast(F32)
+        def w_turn(i):
+            w_ps[i] = psum.tile([P, PASSES, 2, P], F32, name="wps%d" % i, tag="bank")
+            words = w_raw[M_ORDER[i]][:].bitcast(F32)
             for g in range(PASSES):
                 for u in range(2):
-                    nc.tensor.transpose(w_ps[m][:, g, u, :], words[:, 256 * g + u:256 * (g + 1):2], ident[:])
+                    nc.tensor.transpose(w_ps[i][:, g, u, :], words[:, 256 * g + u:256 * (g + 1):2], ident[:])
 
-        def w_out(m, who):
-            dst = w_grp[m][:].bitcast(F32).rearrange("p (g r u) -> p g r u", g=PASSES, u=2)
-            src = w_ps[m][:].rearrange("p g u r -> p g r u")
+        def w_out(i, who):
+            dst = w_grp[:, i, :].bitcast(F32).rearrange("p (g r u) -> p g r u", g=PASSES, u=2)
+            src = w_ps[i][:].rearrange("p g u r -> p g r u")
             if who == "V":
                 nc.vector.tensor_copy(out=dst, in_=src)
             else:
                 nc.scalar.copy(out=dst, in_=src)
 
-        def w_quant(m):
-            nc.vector.quantize_mx(out=w_cod[m][:].bitcast(FP8X4), scales=w_scl[m][:], in_=w_grp[m][:])
+        def w_quant(i0, i1):
+            nc.vector.quantize_mx(
+                out=w_cod[:, i0:i1, :].rearrange("p i n -> p (i n)").bitcast(FP8X4),
+                scales=w_scl[:, i0:i1, :].rearrange("p i n -> p (i n)"),
+                in_=w_grp[:, i0:i1, :].rearrange("p i n -> p (i n)"),
+            )
 
-        def mult(c, m):
-            acc[c, m] = psum.tile([P, CH], F32, name="acc%d%d" % (c, m), tag="bank")
+        def mult(c, i):
+            acc[c, i] = psum.tile([P, CH], F32, name="acc%d%d" % (c, i), tag="bank")
             for g in range(PASSES):
                 rows = slice(g * P, (g + 1) * P)
                 nc.tensor.matmul_mx(
-                    out=acc[c, m][:],
-                    lhsT=w_cod[m][:, rows].bitcast(FP8X4),
-                    lhsT_scale=w_scl[m][:, rows],
-                    rhs=xc[c, g][:].bitcast(FP8X4),
-                    rhs_scale=xs[c, g][:],
+                    out=acc[c, i][:],
+                    lhsT=w_cod[:, i, rows].bitcast(FP8X4),
+                    lhsT_scale=w_scl[:, i, rows],
+                    rhs=xc[c][:, g, :].bitcast(FP8X4),
+                    rhs_scale=xs[c][:, g, :],
                     start=(g == 0),
                     stop=(g == PASSES - 1),
                 )
 
-        def pool(c, m):
+        def pool(c, i):
             nc.vector.tensor_reduce(
-                out=kv_sb[c][:, m - 1, :],
-                in_=acc[c, m][:].rearrange("p (w j) -> p w j", j=WIN),
+                out=kv_sb[c][:, i, :],
+                in_=acc[c, i][:].rearrange("p (w j) -> p w j", j=WIN),
                 axis=AX.X,
                 op=ALU.max,
             )
@@ -160,80 +178,88 @@ def tile_selfattention_pa_kernel(tc, x_bytes, x_scale, Wq, Wk, Wv, out_0, out_1,
             nc.sync.dma_start(out=v_out[:, :, cols], in_=kv_sb[c][:, 1:MT - 1, :])
 
         def q_copy(c):
-            nc.scalar.copy(out=q_sb[c][:], in_=acc[c, 0][:])
+            nc.scalar.copy(out=q_sb[c][:], in_=acc[c, MT - 1][:])
             nc.sync.dma_start(out=q_out[:, c * CH:(c + 1) * CH], in_=q_sb[c][:])
 
+        NP = MT - 1
+        QPOS = 2
+
         with tc.manual_schedule():
-            nc.sync.dma_start(out=scale[:], in_=s_rows)
+            nc.scalar.dma_start(out=scale[:], in_=s_rows)
             load_x(0, 0)
             load_x(0, 1)
-            for m in (0, 1, 2):
-                load_w(m)
-            load_x(1, G_G)
-            load_x(1, G_V)
-            for m in (3, 4, 5):
-                load_w(m)
-            for c in (2, 3):
-                load_x(c, G_G)
-                load_x(c, G_V)
+            for i in (0, 1, 2):
+                load_w(M_ORDER[i])
+            load_x(1, 0)
+            for i in (3, 4):
+                load_w(M_ORDER[i])
+            load_x(1, 1)
+            load_x(2, 0)
+            load_x(2, 1)
+            load_x(3, 1)
+            load_x(3, 0)
+            load_w(M_ORDER[NP])
             nc.scalar.activation(out=warm[:, 1:2], in_=warm[:, 0:1], func=ACT.Copy, scale=1.0)
 
             for g in range(PASSES):
                 widen(0, g, "S")
                 widen(0, g, "V")
+            inter(0, 0, "T")
+            inter(0, 1, "T")
             inter(0, 0, "V")
-            inter(0, 0, "S")
-            quant(0, 0)
-            inter(0, 1, "S")
             inter(0, 1, "V")
-            for m in (0, 1, 2):
-                w_turn(m)
-            w_out(0, "V")
-            w_out(1, "V")
-            w_out(2, "S")
-            quant(0, 1)
-            for m in (0, 1, 2):
-                w_quant(m)
-            widen(1, G_G, "S")
-            widen(1, G_G, "V")
-            inter(1, G_G, "G")
-            widen(1, G_V, "V")
-            for m in (3, 4, 5):
-                w_turn(m)
-                w_out(m, "S")
-            for m in (1, 2):
-                mult(0, m)
-                pool(0, m)
-            for m in (3, 4, 5):
-                w_quant(m)
-            for m in (3, 4, 5):
-                mult(0, m)
-                pool(0, m)
-            mult(0, 0)
+            inter_out(0, 0, "S")
+            inter_out(0, 1, "S")
+            quant(0)
+            for i in (0, 1):
+                w_turn(i)
+                w_out(i, "S")
+            w_quant(0, 2)
+            widen(1, 0, "V")
+            for i in (2, 3, 4):
+                w_turn(i)
+                w_out(i, "S")
+            w_quant(2, 4)
+            w_quant(4, 5)
+            widen(2, 0, "V")
+            widen(1, 1, "S")
+            widen(1, 1, "V")
+            inter(1, 1, "G")
+            widen(1, 0, "S")
+            for i in range(NP):
+                mult(0, i)
+            inter(1, 0, "T")
+            for i in range(NP):
+                pool(0, i)
             store_kv(0)
-            widen(1, G_V, "S")
-            inter(1, G_G, "S")
-            inter(1, G_V, "S")
-            widen(2, G_G, "S")
+            widen(2, 1, "S")
+            inter_out(1, 0, "S")
+            widen(2, 0, "S")
 
             for s in range(1, NCH):
-                inter(s, G_G, "V")
-                inter(s, G_V, "V")
-                quant(s, G_G)
-                quant(s, G_V)
                 if s + 1 < NCH:
-                    widen(s + 1, G_G, "V")
-                    widen(s + 1, G_V, "V")
-                    inter(s + 1, G_G, "G")
-                    widen(s + 1, G_V, "S")
-                    inter(s + 1, G_G, "S")
-                    inter(s + 1, G_V, "S")
-                q_copy(s - 1)
+                    inter(s + 1, 0, "T")
+                quant(s)
+                if s == NCH - 2:
+                    w_quant(NP, MT)
+                if s + 1 < NCH:
+                    widen(s + 1, 1, "V")
+                    inter(s + 1, 1, "G")
+                    inter_out(s + 1, 0, "S")
                 if s + 2 < NCH:
-                    widen(s + 2, G_G, "S")
-                for m in (1, 2, 3, 4, 5):
-                    mult(s, m)
-                    pool(s, m)
-                mult(s, 0)
+                    widen(s + 2, 1, "S")
+                    widen(s + 2, 0, "S")
+                for i in range(NP):
+                    mult(s, i)
+                    pool(s, i)
+                    if s == NCH - 1 and i == QPOS:
+                        mult(s, NP)
+                        q_copy(s)
+                if s == 1:
+                    w_turn(NP)
+                    w_out(NP, "S")
                 store_kv(s)
-            q_copy(NCH - 1)
+                if s == NCH - 2:
+                    for c in range(NCH - 1):
+                        mult(c, NP)
+                        q_copy(c)

@@ -26,8 +26,8 @@ WIN = 4
 MT = 6
 M_ORDER = (1, 2, 3, 4, 5, 0)
 
-WIDEN = (("SVVV", "SSVV"), ("SSVV", "SSVV"), ("SSVV", "SSVV"), ("SSSS", "SSVV"))
-INTER = (("VT", "VT"), ("TT", "GG"), ("TT", "GG"), ("TT", "GG"))
+WIDEN = (("SSVV", "SSVV"), ("SSSS", "VVVV"), ("SSSS", "SSVV"), ("SSSS", "SSVV"))
+INTER = (("VV", "SV"), ("SV", "GV"), ("SV", "GG"), ("SV", "GG"))
 
 
 def tile_selfattention_pa_kernel(tc, x_bytes, x_scale, Wq, Wk, Wv, out_0, out_1, out_2):
@@ -77,8 +77,8 @@ def tile_selfattention_pa_kernel(tc, x_bytes, x_scale, Wq, Wk, Wv, out_0, out_1,
         def load_w(m):
             nc.sync.dma_start(out=w_raw[m][:], in_=w_src[m])
 
-        def widen(c, g, who):
-            for t in range(PACK):
+        def widen(c, g, who, planes=(0, 1, 2, 3)):
+            for t in planes:
                 if WIDEN[c][g][t] == who:
                     src = xb[c, g][:, t, :].bitcast(FP8)
                     dst = wide[c, g][:, t, :]
@@ -182,7 +182,7 @@ def tile_selfattention_pa_kernel(tc, x_bytes, x_scale, Wq, Wk, Wv, out_0, out_1,
             nc.sync.dma_start(out=q_out[:, c * CH:(c + 1) * CH], in_=q_sb[c][:])
 
         NP = MT - 1
-        QPOS = 2
+        LAG = 2
 
         with tc.manual_schedule():
             nc.scalar.dma_start(out=scale[:], in_=s_rows)
@@ -190,12 +190,12 @@ def tile_selfattention_pa_kernel(tc, x_bytes, x_scale, Wq, Wk, Wv, out_0, out_1,
             load_x(0, 1)
             for i in (0, 1, 2):
                 load_w(M_ORDER[i])
-            load_x(1, 0)
+            load_x(1, 1)
             for i in (3, 4):
                 load_w(M_ORDER[i])
-            load_x(1, 1)
-            load_x(2, 0)
+            load_x(1, 0)
             load_x(2, 1)
+            load_x(2, 0)
             load_x(3, 1)
             load_x(3, 0)
             load_w(M_ORDER[NP])
@@ -204,62 +204,65 @@ def tile_selfattention_pa_kernel(tc, x_bytes, x_scale, Wq, Wk, Wv, out_0, out_1,
             for g in range(PASSES):
                 widen(0, g, "S")
                 widen(0, g, "V")
-            inter(0, 0, "T")
-            inter(0, 1, "T")
             inter(0, 0, "V")
+            inter(0, 0, "S")
+            inter(0, 1, "S")
             inter(0, 1, "V")
-            inter_out(0, 0, "S")
-            inter_out(0, 1, "S")
-            quant(0)
             for i in (0, 1):
                 w_turn(i)
                 w_out(i, "S")
+            quant(0)
             w_quant(0, 2)
-            widen(1, 0, "V")
+            widen(1, 1, "V", (0, 1))
             for i in (2, 3, 4):
                 w_turn(i)
                 w_out(i, "S")
+            widen(1, 1, "S")
             w_quant(2, 4)
             w_quant(4, 5)
-            widen(2, 0, "V")
-            widen(1, 1, "S")
-            widen(1, 1, "V")
+            widen(1, 0, "V")
+            widen(1, 1, "V", (2, 3))
             inter(1, 1, "G")
-            widen(1, 0, "S")
             for i in range(NP):
                 mult(0, i)
-            inter(1, 0, "T")
-            for i in range(NP):
+            for i in range(NP - LAG):
                 pool(0, i)
-            store_kv(0)
-            widen(2, 1, "S")
-            inter_out(1, 0, "S")
-            widen(2, 0, "S")
+            widen(1, 0, "S")
+            inter(1, 0, "S")
+            inter(1, 1, "S")
 
             for s in range(1, NCH):
-                if s + 1 < NCH:
-                    inter(s + 1, 0, "T")
+                inter(s, 1, "V")
+                inter(s, 0, "V")
                 quant(s)
                 if s == NCH - 2:
                     w_quant(NP, MT)
                 if s + 1 < NCH:
+                    widen(s + 1, 0, "V")
+                    widen(s + 1, 1, "S")
                     widen(s + 1, 1, "V")
                     inter(s + 1, 1, "G")
-                    inter_out(s + 1, 0, "S")
-                if s + 2 < NCH:
-                    widen(s + 2, 1, "S")
-                    widen(s + 2, 0, "S")
+                for i in range(NP - LAG, NP):
+                    pool(s - 1, i)
+                store_kv(s - 1)
                 for i in range(NP):
                     mult(s, i)
+                if s == NCH - 1:
+                    mult(s, NP)
+                    q_copy(s)
+                for i in range(NP - LAG):
                     pool(s, i)
-                    if s == NCH - 1 and i == QPOS:
-                        mult(s, NP)
-                        q_copy(s)
+                if s + 1 < NCH:
+                    widen(s + 1, 0, "S")
+                    inter(s + 1, 0, "S")
+                    inter(s + 1, 1, "S")
                 if s == 1:
                     w_turn(NP)
                     w_out(NP, "S")
-                store_kv(s)
                 if s == NCH - 2:
                     for c in range(NCH - 1):
                         mult(c, NP)
                         q_copy(c)
+            for i in range(NP - LAG, NP):
+                pool(NCH - 1, i)
+            store_kv(NCH - 1)

@@ -94,10 +94,12 @@ def tile_selfattention_pa_kernel(tc, x_bytes, x_scale, Wq, Wk, Wv, out_0, out_1,
                     cols = slice(h * HALF, (h + 1) * HALF)
                     dst = grp[c][:, g, cols, :]
                     src = wide[c, g][:, :, cols].rearrange("p t n -> p n t")
+                    dst4 = dst.rearrange("p (c i) t -> p c t i", i=4)
+                    src4 = wide[c, g][:, :, cols].rearrange("p t (c i) -> p c t i", i=4)
                     if who == "V":
-                        nc.vector.tensor_copy(out=dst, in_=src)
+                        nc.vector.tensor_copy(out=dst4, in_=src4)
                     elif who == "S":
-                        nc.scalar.copy(out=dst, in_=src)
+                        nc.scalar.copy(out=dst4, in_=src4)
                     elif who == "G":
                         nc.gpsimd.tensor_scalar(out=dst, in0=src, scalar1=1.0, scalar2=0.0, op0=ALU.mult, op1=ALU.add)
                     else:

@@ -11,31 +11,34 @@ U32 = mybir.dt.uint32
 U8 = mybir.dt.uint8
 FP8 = mybir.dt.float8_e4m3fn
 FP8X4 = mybir.dt.float8_e4m3fn_x4
-ACT = mybir.ActivationFunctionType
-ALU = mybir.AluOpType
-AX = mybir.AxisListType
+COPY = mybir.ActivationFunctionType.Copy
+MULT = mybir.AluOpType.mult
+ADD = mybir.AluOpType.add
+MAX = mybir.AluOpType.max
 
 P = 128
 PACK = 4
 PASSES = 2
-T_ALL = 2048
-CH = 512
-NCH = T_ALL // CH
-HALF = CH // 2
-WIN = 4
-MT = 6
-M_ORDER = (1, 2, 3, 4, 5, 0)
-
-WIDEN = (("SSVV", "SSVV"), ("SSSS", "VVVV"), ("SSSS", "SSVV"), ("SSSS", "SSVV"))
-INTER = (("VV", "SV"), ("SV", "GV"), ("SV", "GG"), ("SV", "GG"))
+K_PASS = P * PACK
+CHUNK = 512
+N_CHUNKS = 4
+HALF = CHUNK // 2
+WINDOW = 4
+POOLED = CHUNK // WINDOW
+ROW_TILES = 6
+N_KV = ROW_TILES - 1
+Q_TILE = ROW_TILES - 1
+LAG = 3
+Q_AFTER = 2
+ALL_PLANES = (0, 1, 2, 3)
 
 
 def tile_selfattention_pa_kernel(tc, x_bytes, x_scale, Wq, Wk, Wv, out_0, out_1, out_2):
     nc = tc.nc
     x_rows = x_bytes.flatten_outer_dims().rearrange("(g p t) n -> g p t n", p=P, t=PACK)
-    s_rows = x_scale.flatten_outer_dims().rearrange("(g p t) o -> p g (t o)", p=P, t=PACK)
+    scale_rows = x_scale.flatten_outer_dims().rearrange("(g p t) o -> p g (t o)", p=P, t=PACK)
     wv_rows = Wv.rearrange("(m p) k -> m p k", p=P)
-    w_src = [Wq, Wk] + [wv_rows[i] for i in range(4)]
+    w_rows = [Wk] + [wv_rows[m] for m in range(4)] + [Wq]
     q_out = out_0.flatten_outer_dims()
     k_out = out_1.flatten_outer_dims()
     v_out = out_2.flatten_outer_dims().rearrange("(m p) w -> p m w", p=P)
@@ -46,122 +49,98 @@ def tile_selfattention_pa_kernel(tc, x_bytes, x_scale, Wq, Wk, Wv, out_0, out_1,
 
         ident = keep.tile([P, P], F32, name="ident")
         make_identity(nc, ident[:])
-        ident_bf = keep.tile([P, P], BF16, name="identbf")
-        make_identity(nc, ident_bf[:])
         warm = keep.tile([P, 2], F32, name="warm")
         nc.vector.memset(warm[:], 0.0)
 
         scale = keep.tile([P, PASSES, PACK], F32, name="scale")
-        xb = {}
-        wide = {}
-        for c in range(NCH):
+        x_raw = {}
+        x_wide = {}
+        for c in range(N_CHUNKS):
             for g in range(PASSES):
-                xb[c, g] = keep.tile([P, PACK, CH], U8, name="xbytes%d%d" % (c, g))
-                wide[c, g] = keep.tile([P, PACK, CH], BF16, name="wide%d%d" % (c, g))
-        grp = [keep.tile([P, PASSES, CH, PACK], BF16, name="grp%d" % c, align_bytes=64) for c in range(NCH)]
-        xc = [keep.tile([P, PASSES, CH], U32, name="xcodes%d" % c, align_bytes=64) for c in range(NCH)]
-        xs = [keep.tile([P, PASSES, CH], U8, name="xscales%d" % c, align_bytes=64) for c in range(NCH)]
-        w_raw = [keep.tile([P, PASSES * 512], BF16, name="wraw%d" % m) for m in range(MT)]
-        w_grp = keep.tile([P, MT, PASSES * 512], BF16, name="wgrp", align_bytes=64)
-        w_cod = keep.tile([P, MT, PASSES * P], U32, name="wcodes", align_bytes=64)
-        w_scl = keep.tile([P, MT, PASSES * P], U8, name="wscales", align_bytes=64)
-        q_sb = [keep.tile([P, CH], F32, name="qsb%d" % c) for c in range(NCH)]
-        kv_sb = [keep.tile([P, MT - 1, CH // WIN], F32, name="kvsb%d" % c) for c in range(NCH)]
-        w_ps = {}
+                x_raw[c, g] = keep.tile([P, PACK, CHUNK], U8, name="xraw%d%d" % (c, g))
+                x_wide[c, g] = keep.tile([P, PACK, CHUNK], BF16, name="xwide%d%d" % (c, g))
+        x_grouped = [
+            keep.tile([P, PASSES, CHUNK, PACK], BF16, name="xgrouped%d" % c, align_bytes=64) for c in range(N_CHUNKS)
+        ]
+        x_codes = [keep.tile([P, PASSES, CHUNK], U32, name="xcodes%d" % c, align_bytes=64) for c in range(N_CHUNKS)]
+        x_scales = [keep.tile([P, PASSES, CHUNK], U8, name="xscales%d" % c, align_bytes=64) for c in range(N_CHUNKS)]
+        w_raw = [keep.tile([P, PASSES * K_PASS], BF16, name="wraw%d" % i) for i in range(ROW_TILES)]
+        w_grouped = keep.tile([P, ROW_TILES, PASSES * K_PASS], BF16, name="wgrouped", align_bytes=64)
+        w_codes = keep.tile([P, ROW_TILES, PASSES * P], U32, name="wcodes", align_bytes=64)
+        w_scales = keep.tile([P, ROW_TILES, PASSES * P], U8, name="wscales", align_bytes=64)
+        q_sb = [keep.tile([P, CHUNK], F32, name="qsb%d" % c) for c in range(N_CHUNKS)]
+        kv_sb = [keep.tile([P, N_KV, POOLED], F32, name="kvsb%d" % c) for c in range(N_CHUNKS)]
+        w_turned = {}
         acc = {}
-        il_ps = {}
 
         def load_x(c, g):
-            nc.sync.dma_start(out=xb[c, g][:], in_=x_rows[g][:, :, c * CH:(c + 1) * CH])
+            nc.sync.dma_start(out=x_raw[c, g][:], in_=x_rows[g][:, :, c * CHUNK:(c + 1) * CHUNK])
 
-        def load_w(m):
-            nc.sync.dma_start(out=w_raw[m][:], in_=w_src[m])
+        def load_w(i):
+            nc.sync.dma_start(out=w_raw[i][:], in_=w_rows[i])
 
-        def widen(c, g, who, planes=(0, 1, 2, 3)):
+        def widen(engine, c, g, planes):
             for t in planes:
-                if WIDEN[c][g][t] == who:
-                    src = xb[c, g][:, t, :].bitcast(FP8)
-                    dst = wide[c, g][:, t, :]
-                    col = scale[:, g, t:t + 1]
-                    if who == "S":
-                        nc.scalar.activation(out=dst, in_=src, func=ACT.Copy, scale=col)
-                    else:
-                        nc.vector.tensor_scalar(out=dst, in0=src, scalar1=col, scalar2=None, op0=ALU.mult)
+                src = x_raw[c, g][:, t, :].bitcast(FP8)
+                dst = x_wide[c, g][:, t, :]
+                if engine is nc.scalar:
+                    nc.scalar.activation(out=dst, in_=src, func=COPY, scale=scale[:, g, t:t + 1])
+                else:
+                    nc.vector.tensor_scalar(out=dst, in0=src, scalar1=scale[:, g, t:t + 1], scalar2=None, op0=MULT)
 
-        def inter(c, g, who):
-            for h in range(2):
-                if INTER[c][g][h] == who:
-                    cols = slice(h * HALF, (h + 1) * HALF)
-                    dst = grp[c][:, g, cols, :]
-                    src = wide[c, g][:, :, cols].rearrange("p t n -> p n t")
-                    dst4 = dst.rearrange("p (c i) t -> p c t i", i=4)
-                    src4 = wide[c, g][:, :, cols].rearrange("p t (c i) -> p c t i", i=4)
-                    if who == "V":
-                        nc.vector.tensor_copy(out=dst4, in_=src4)
-                    elif who == "S":
-                        nc.scalar.copy(out=dst4, in_=src4)
-                    elif who == "G":
-                        nc.gpsimd.tensor_scalar(out=dst, in0=src, scalar1=1.0, scalar2=0.0, op0=ALU.mult, op1=ALU.add)
-                    else:
-                        il_ps[c, g, h] = psum.tile([P, HALF, PACK], BF16, name="ilps%d%d%d" % (c, g, h), tag="bank")
-                        for j in range(2):
-                            part = slice(j * P, (j + 1) * P)
-                            nc.tensor.matmul(
-                                out=il_ps[c, g, h][:, part, :],
-                                lhsT=ident_bf[:],
-                                rhs=src[:, part, :],
-                                start=True,
-                                stop=True,
-                            )
+        def interleave(engine, c, g, h):
+            cols = slice(h * HALF, (h + 1) * HALF)
+            src = x_wide[c, g][:, :, cols]
+            dst = x_grouped[c][:, g, cols, :]
+            if engine is nc.gpsimd:
+                nc.gpsimd.tensor_scalar(
+                    out=dst, in0=src.rearrange("p t n -> p n t"), scalar1=1.0, scalar2=0.0, op0=MULT, op1=ADD
+                )
+            else:
+                src_runs = src.rearrange("p t (b i) -> p b t i", i=4)
+                dst_runs = dst.rearrange("p (b i) t -> p b t i", i=4)
+                if engine is nc.scalar:
+                    nc.scalar.copy(out=dst_runs, in_=src_runs)
+                else:
+                    nc.vector.tensor_copy(out=dst_runs, in_=src_runs)
 
-        def inter_out(c, g, who):
-            for h in range(2):
-                if INTER[c][g][h] == "T":
-                    cols = slice(h * HALF, (h + 1) * HALF)
-                    if who == "S":
-                        nc.scalar.copy(out=grp[c][:, g, cols, :], in_=il_ps[c, g, h][:])
-                    else:
-                        nc.vector.tensor_copy(out=grp[c][:, g, cols, :], in_=il_ps[c, g, h][:])
-
-        def quant(c):
+        def quantize_x(c):
             nc.vector.quantize_mx(
-                out=xc[c][:].rearrange("p g n -> p (g n)").bitcast(FP8X4),
-                scales=xs[c][:].rearrange("p g n -> p (g n)"),
-                in_=grp[c][:].rearrange("p g n t -> p (g n t)"),
+                out=x_codes[c][:].rearrange("p g n -> p (g n)").bitcast(FP8X4),
+                scales=x_scales[c][:].rearrange("p g n -> p (g n)"),
+                in_=x_grouped[c][:].rearrange("p g n t -> p (g n t)"),
             )
 
-        def w_turn(i):
-            w_ps[i] = psum.tile([P, PASSES, 2, P], F32, name="wps%d" % i, tag="bank")
-            words = w_raw[M_ORDER[i]][:].bitcast(F32)
+        def turn_w(i):
+            w_turned[i] = psum.tile([P, PASSES, 2, P], F32, name="wturned%d" % i, tag="bank")
+            words = w_raw[i][:].bitcast(F32)
             for g in range(PASSES):
                 for u in range(2):
-                    nc.tensor.transpose(w_ps[i][:, g, u, :], words[:, 256 * g + u:256 * (g + 1):2], ident[:])
+                    nc.tensor.transpose(w_turned[i][:, g, u, :], words[:, 256 * g + u:256 * (g + 1):2], ident[:])
 
-        def w_out(i, who):
-            dst = w_grp[:, i, :].bitcast(F32).rearrange("p (g r u) -> p g r u", g=PASSES, u=2)
-            src = w_ps[i][:].rearrange("p g u r -> p g r u")
-            if who == "V":
-                nc.vector.tensor_copy(out=dst, in_=src)
-            else:
-                nc.scalar.copy(out=dst, in_=src)
-
-        def w_quant(i0, i1):
-            nc.vector.quantize_mx(
-                out=w_cod[:, i0:i1, :].rearrange("p i n -> p (i n)").bitcast(FP8X4),
-                scales=w_scl[:, i0:i1, :].rearrange("p i n -> p (i n)"),
-                in_=w_grp[:, i0:i1, :].rearrange("p i n -> p (i n)"),
+        def copy_w(i):
+            nc.scalar.copy(
+                out=w_grouped[:, i, :].bitcast(F32).rearrange("p (g r u) -> p g r u", g=PASSES, u=2),
+                in_=w_turned[i][:].rearrange("p g u r -> p g r u"),
             )
 
-        def mult(c, i):
-            acc[c, i] = psum.tile([P, CH], F32, name="acc%d%d" % (c, i), tag="bank")
+        def quantize_w(i0, i1):
+            nc.vector.quantize_mx(
+                out=w_codes[:, i0:i1, :].rearrange("p i n -> p (i n)").bitcast(FP8X4),
+                scales=w_scales[:, i0:i1, :].rearrange("p i n -> p (i n)"),
+                in_=w_grouped[:, i0:i1, :].rearrange("p i n -> p (i n)"),
+            )
+
+        def multiply(c, i):
+            acc[c, i] = psum.tile([P, CHUNK], F32, name="acc%d%d" % (c, i), tag="bank")
             for g in range(PASSES):
                 rows = slice(g * P, (g + 1) * P)
                 nc.tensor.matmul_mx(
                     out=acc[c, i][:],
-                    lhsT=w_cod[:, i, rows].bitcast(FP8X4),
-                    lhsT_scale=w_scl[:, i, rows],
-                    rhs=xc[c][:, g, :].bitcast(FP8X4),
-                    rhs_scale=xs[c][:, g, :],
+                    lhsT=w_codes[:, i, rows].bitcast(FP8X4),
+                    lhsT_scale=w_scales[:, i, rows],
+                    rhs=x_codes[c][:, g, :].bitcast(FP8X4),
+                    rhs_scale=x_scales[c][:, g, :],
                     start=(g == 0),
                     stop=(g == PASSES - 1),
                 )
@@ -169,102 +148,101 @@ def tile_selfattention_pa_kernel(tc, x_bytes, x_scale, Wq, Wk, Wv, out_0, out_1,
         def pool(c, i):
             nc.vector.tensor_reduce(
                 out=kv_sb[c][:, i, :],
-                in_=acc[c, i][:].rearrange("p (w j) -> p w j", j=WIN),
-                axis=AX.X,
-                op=ALU.max,
+                in_=acc[c, i][:].rearrange("p (w j) -> p w j", j=WINDOW),
+                axis=mybir.AxisListType.X,
+                op=MAX,
             )
 
-        def store_kv(c):
-            cols = slice(c * (CH // WIN), (c + 1) * (CH // WIN))
+        def pool_first(c):
+            for i in range(N_KV - LAG):
+                pool(c, i)
+            cols = slice(c * POOLED, (c + 1) * POOLED)
             nc.sync.dma_start(out=k_out[:, cols], in_=kv_sb[c][:, 0, :])
-            nc.sync.dma_start(out=v_out[:, :, cols], in_=kv_sb[c][:, 1:MT - 1, :])
+            nc.sync.dma_start(out=v_out[:, 0:N_KV - LAG - 1, cols], in_=kv_sb[c][:, 1:N_KV - LAG, :])
 
-        def q_copy(c):
-            nc.scalar.copy(out=q_sb[c][:], in_=acc[c, MT - 1][:])
-            nc.sync.dma_start(out=q_out[:, c * CH:(c + 1) * CH], in_=q_sb[c][:])
+        def pool_rest(c):
+            for i in range(N_KV - LAG, N_KV):
+                pool(c, i)
+            cols = slice(c * POOLED, (c + 1) * POOLED)
+            nc.sync.dma_start(out=v_out[:, N_KV - LAG - 1:N_KV - 1, cols], in_=kv_sb[c][:, N_KV - LAG:N_KV, :])
 
-        NP = MT - 1
-        LAG = 2
+        def project_q(c):
+            multiply(c, Q_TILE)
+            nc.scalar.copy(out=q_sb[c][:], in_=acc[c, Q_TILE][:])
+            nc.sync.dma_start(out=q_out[:, c * CHUNK:(c + 1) * CHUNK], in_=q_sb[c][:])
 
         with tc.manual_schedule():
-            nc.scalar.dma_start(out=scale[:], in_=s_rows)
+            nc.scalar.dma_start(out=scale[:], in_=scale_rows)
             load_x(0, 0)
             load_x(0, 1)
             for i in (0, 1, 2):
-                load_w(M_ORDER[i])
+                load_w(i)
             load_x(1, 1)
             for i in (3, 4):
-                load_w(M_ORDER[i])
+                load_w(i)
             load_x(1, 0)
-            load_x(2, 1)
-            load_x(2, 0)
-            load_x(3, 1)
-            load_x(3, 0)
-            load_w(M_ORDER[NP])
-            nc.scalar.activation(out=warm[:, 1:2], in_=warm[:, 0:1], func=ACT.Copy, scale=1.0)
+            for c in (2, 3):
+                load_x(c, 1)
+                load_x(c, 0)
+            load_w(Q_TILE)
+            nc.scalar.activation(out=warm[:, 1:2], in_=warm[:, 0:1], func=COPY, scale=1.0)
 
             for g in range(PASSES):
-                widen(0, g, "S")
-                widen(0, g, "V")
-            inter(0, 0, "V")
-            inter(0, 0, "S")
-            inter(0, 1, "S")
-            inter(0, 1, "V")
+                widen(nc.scalar, 0, g, (0, 1))
+                widen(nc.vector, 0, g, (2, 3))
+            interleave(nc.vector, 0, 0, 0)
+            interleave(nc.vector, 0, 0, 1)
+            interleave(nc.scalar, 0, 1, 0)
+            interleave(nc.vector, 0, 1, 1)
             for i in (0, 1):
-                w_turn(i)
-                w_out(i, "S")
-            quant(0)
-            w_quant(0, 2)
-            widen(1, 1, "V", (0, 1))
+                turn_w(i)
+                copy_w(i)
+            quantize_x(0)
+            quantize_w(0, 2)
+            widen(nc.vector, 1, 1, (0, 1))
             for i in (2, 3, 4):
-                w_turn(i)
-                w_out(i, "S")
-            widen(1, 1, "S")
-            w_quant(2, 4)
-            w_quant(4, 5)
-            widen(1, 0, "V")
-            widen(1, 1, "V", (2, 3))
-            inter(1, 1, "G")
-            for i in range(NP):
-                mult(0, i)
-            for i in range(NP - LAG):
-                pool(0, i)
-            widen(1, 0, "S")
-            inter(1, 0, "S")
-            inter(1, 1, "S")
+                turn_w(i)
+                copy_w(i)
+            quantize_w(2, 4)
+            quantize_w(4, 5)
+            widen(nc.vector, 1, 1, (2, 3))
+            interleave(nc.gpsimd, 1, 1, 0)
+            for i in range(N_KV):
+                multiply(0, i)
+            pool_first(0)
+            widen(nc.scalar, 1, 0, ALL_PLANES)
+            interleave(nc.scalar, 1, 0, 0)
+            turn_w(Q_TILE)
+            copy_w(Q_TILE)
 
-            for s in range(1, NCH):
-                inter(s, 1, "V")
-                inter(s, 0, "V")
-                quant(s)
-                if s == NCH - 2:
-                    w_quant(NP, MT)
-                if s + 1 < NCH:
-                    widen(s + 1, 0, "V")
-                    widen(s + 1, 1, "S")
-                    widen(s + 1, 1, "V")
-                    inter(s + 1, 1, "G")
-                for i in range(NP - LAG, NP):
-                    pool(s - 1, i)
-                store_kv(s - 1)
-                for i in range(NP):
-                    mult(s, i)
-                if s == NCH - 1:
-                    mult(s, NP)
-                    q_copy(s)
-                for i in range(NP - LAG):
-                    pool(s, i)
-                if s + 1 < NCH:
-                    widen(s + 1, 0, "S")
-                    inter(s + 1, 0, "S")
-                    inter(s + 1, 1, "S")
-                if s == 1:
-                    w_turn(NP)
-                    w_out(NP, "S")
-                if s == NCH - 2:
-                    for c in range(NCH - 1):
-                        mult(c, NP)
-                        q_copy(c)
-            for i in range(NP - LAG, NP):
-                pool(NCH - 1, i)
-            store_kv(NCH - 1)
+            for c in range(1, N_CHUNKS):
+                nxt = c + 1
+                if c == 1:
+                    interleave(nc.vector, c, 1, 1)
+                if c < N_CHUNKS - 1:
+                    interleave(nc.vector, c, 0, 1)
+                if nxt < N_CHUNKS:
+                    widen(nc.vector, nxt, 1, (2,))
+                quantize_x(c)
+                if c == N_CHUNKS - 2:
+                    quantize_w(Q_TILE, ROW_TILES)
+                if nxt < N_CHUNKS:
+                    widen(nc.scalar, nxt, 1, (0, 1))
+                    widen(nc.vector, nxt, 1, (3,))
+                    interleave(nc.gpsimd, nxt, 1, 0)
+                    interleave(nc.gpsimd, nxt, 1, 1)
+                pool_rest(c - 1)
+                for i in range(N_KV):
+                    if c == N_CHUNKS - 1 and i == Q_AFTER:
+                        project_q(c)
+                    multiply(c, i)
+                pool_first(c)
+                if nxt < N_CHUNKS:
+                    widen(nc.scalar, nxt, 0, ALL_PLANES)
+                    interleave(nc.scalar, nxt, 0, 0)
+                    if nxt == N_CHUNKS - 1:
+                        interleave(nc.scalar, nxt, 0, 1)
+                if c == N_CHUNKS - 2:
+                    for done in range(N_CHUNKS - 1):
+                        project_q(done)
+            pool_rest(N_CHUNKS - 1)

@@ -70,6 +70,8 @@ def tile_selfattention_pa_kernel(tc, x_bytes, x_scale, Wq, Wk, Wv, out_0, out_1,
         w_scales = keep.tile([P, ROW_TILES, PASSES * P], U8, name="wscales", align_bytes=64)
         q_sb = [keep.tile([P, CHUNK], F32, name="qsb%d" % c) for c in range(N_CHUNKS)]
         kv_sb = [keep.tile([P, N_KV, POOLED], F32, name="kvsb%d" % c) for c in range(N_CHUNKS)]
+        late_half = keep.tile([P, LAG, 2, POOLED], F32, name="latehalf")
+        late_max = keep.tile([P, LAG, 2, POOLED], F32, name="latemax")
         w_turned = {}
         acc = {}
 
@@ -88,8 +90,8 @@ def tile_selfattention_pa_kernel(tc, x_bytes, x_scale, Wq, Wk, Wv, out_0, out_1,
                 else:
                     nc.vector.tensor_scalar(out=dst, in0=src, scalar1=scale[:, g, t:t + 1], scalar2=None, op0=MULT)
 
-        def interleave(engine, c, g, h):
-            cols = slice(h * HALF, (h + 1) * HALF)
+        def interleave(engine, c, g, h, halves=1):
+            cols = slice(h * HALF, (h + halves) * HALF)
             src = x_wide[c, g][:, :, cols]
             dst = x_grouped[c][:, g, cols, :]
             if engine is nc.gpsimd:
@@ -161,8 +163,29 @@ def tile_selfattention_pa_kernel(tc, x_bytes, x_scale, Wq, Wk, Wv, out_0, out_1,
             nc.sync.dma_start(out=v_out[:, 0:N_KV - LAG - 1, cols], in_=kv_sb[c][:, 1:N_KV - LAG, :])
 
         def pool_rest(c):
-            for i in range(N_KV - LAG, N_KV):
+            cols = slice(c * POOLED, (c + 1) * POOLED)
+            cut = N_KV - 1 if c == N_CHUNKS - 1 else N_KV
+            for i in range(N_KV - LAG, cut):
                 pool(c, i)
+            nc.sync.dma_start(out=v_out[:, N_KV - LAG - 1:cut - 1, cols], in_=kv_sb[c][:, N_KV - LAG:cut, :])
+            for i in range(cut, N_KV):
+                pool(c, i)
+                nc.sync.dma_start(out=v_out[:, i - 1:i, cols], in_=kv_sb[c][:, i:i + 1, :])
+
+        def by_place(c, i):
+            return acc[c, i][:].rearrange("p (w j) -> p j w", j=WINDOW)
+
+        def copy_late_halves(c):
+            for i in range(N_KV - LAG, N_KV):
+                nc.scalar.copy(out=late_half[:, i - (N_KV - LAG), :, :], in_=by_place(c, i)[:, 2:4, :])
+
+        def pool_rest_shared(c):
+            for i in range(N_KV - LAG, N_KV):
+                k = i - (N_KV - LAG)
+                nc.vector.tensor_tensor(out=late_max[:, k, :, :], in0=by_place(c, i)[:, 0:2, :], in1=late_half[:, k, :, :], op=MAX)
+            nc.vector.tensor_tensor(
+                out=kv_sb[c][:, N_KV - LAG:N_KV, :], in0=late_max[:, :, 0, :], in1=late_max[:, :, 1, :], op=MAX
+            )
             cols = slice(c * POOLED, (c + 1) * POOLED)
             nc.sync.dma_start(out=v_out[:, N_KV - LAG - 1:N_KV - 1, cols], in_=kv_sb[c][:, N_KV - LAG:N_KV, :])
 
@@ -190,8 +213,7 @@ def tile_selfattention_pa_kernel(tc, x_bytes, x_scale, Wq, Wk, Wv, out_0, out_1,
             for g in range(PASSES):
                 widen(nc.scalar, 0, g, (0, 1))
                 widen(nc.vector, 0, g, (2, 3))
-            interleave(nc.vector, 0, 0, 0)
-            interleave(nc.vector, 0, 0, 1)
+            interleave(nc.vector, 0, 0, 0, halves=2)
             interleave(nc.scalar, 0, 1, 0)
             interleave(nc.vector, 0, 1, 1)
             for i in (0, 1):
@@ -231,7 +253,10 @@ def tile_selfattention_pa_kernel(tc, x_bytes, x_scale, Wq, Wk, Wv, out_0, out_1,
                     widen(nc.vector, nxt, 1, (3,))
                     interleave(nc.gpsimd, nxt, 1, 0)
                     interleave(nc.gpsimd, nxt, 1, 1)
-                pool_rest(c - 1)
+                if c == N_CHUNKS - 1:
+                    pool_rest_shared(c - 1)
+                else:
+                    pool_rest(c - 1)
                 for i in range(N_KV):
                     if c == N_CHUNKS - 1 and i == Q_AFTER:
                         project_q(c)
@@ -243,6 +268,7 @@ def tile_selfattention_pa_kernel(tc, x_bytes, x_scale, Wq, Wk, Wv, out_0, out_1,
                     if nxt == N_CHUNKS - 1:
                         interleave(nc.scalar, nxt, 0, 1)
                 if c == N_CHUNKS - 2:
+                    copy_late_halves(c)
                     for done in range(N_CHUNKS - 1):
                         project_q(done)
             pool_rest(N_CHUNKS - 1)

@@ -244,12 +244,12 @@ def tile_selfattention_pa_kernel(tc, x_bytes, x_scale, Wq, Wk, Wv, out_0, out_1,
                 if c < N_CHUNKS - 1:
                     interleave(nc.vector, c, 0, 1)
                 if nxt < N_CHUNKS:
-                    widen(nc.vector, nxt, 1, (2,))
+                    widen(nc.vector, nxt, 1, (2,) if nxt == N_CHUNKS - 1 else (1, 2))
                 quantize_x(c)
                 if c == N_CHUNKS - 2:
                     quantize_w(Q_TILE, ROW_TILES)
                 if nxt < N_CHUNKS:
-                    widen(nc.scalar, nxt, 1, (0, 1))
+                    widen(nc.scalar, nxt, 1, (0, 1) if nxt == N_CHUNKS - 1 else (0,))
                     widen(nc.vector, nxt, 1, (3,))
                     interleave(nc.gpsimd, nxt, 1, 0)
                     interleave(nc.gpsimd, nxt, 1, 1)

@@ -251,8 +251,7 @@ def tile_selfattention_pa_kernel(tc, x_bytes, x_scale, Wq, Wk, Wv, out_0, out_1,
                 if nxt < N_CHUNKS:
                     widen(nc.scalar, nxt, 1, (0, 1) if nxt == N_CHUNKS - 1 else (0,))
                     widen(nc.vector, nxt, 1, (3,))
-                    interleave(nc.gpsimd, nxt, 1, 0)
-                    interleave(nc.gpsimd, nxt, 1, 1)
+                    interleave(nc.gpsimd, nxt, 1, 0, halves=2)
                 if c == N_CHUNKS - 1:
                     pool_rest_shared(c - 1)
                 else:
@@ -264,9 +263,7 @@ def tile_selfattention_pa_kernel(tc, x_bytes, x_scale, Wq, Wk, Wv, out_0, out_1,
                 pool_first(c)
                 if nxt < N_CHUNKS:
                     widen(nc.scalar, nxt, 0, ALL_PLANES)
-                    interleave(nc.scalar, nxt, 0, 0)
-                    if nxt == N_CHUNKS - 1:
-                        interleave(nc.scalar, nxt, 0, 1)
+                    interleave(nc.scalar, nxt, 0, 0, halves=2 if nxt == N_CHUNKS - 1 else 1)
                 if c == N_CHUNKS - 2:
                     copy_late_halves(c)
                     for done in range(N_CHUNKS - 1):

@@ -70,8 +70,12 @@ def tile_selfattention_pa_kernel(tc, x_bytes, x_scale, Wq, Wk, Wv, out_0, out_1,
         w_scales = keep.tile([P, ROW_TILES, PASSES * P], U8, name="wscales", align_bytes=64)
         q_sb = [keep.tile([P, CHUNK], F32, name="qsb%d" % c) for c in range(N_CHUNKS)]
         kv_sb = [keep.tile([P, N_KV, POOLED], F32, name="kvsb%d" % c) for c in range(N_CHUNKS)]
-        late_half = keep.tile([P, LAG, 2, POOLED], F32, name="latehalf")
-        late_max = keep.tile([P, LAG, 2, POOLED], F32, name="latemax")
+        late_half = {}
+        late_max = {}
+        for c in (2, 3):
+            late_max[c] = keep.tile([P, N_KV, 2, POOLED], F32, name="latemax%d" % c)
+            for i in range(N_KV):
+                late_half[c, i] = keep.tile([P, 2, POOLED], F32, name="latehalf%d%d" % (c, i))
         w_turned = {}
         acc = {}
 
@@ -113,6 +117,13 @@ def tile_selfattention_pa_kernel(tc, x_bytes, x_scale, Wq, Wk, Wv, out_0, out_1,
                 in_=x_grouped[c][:].rearrange("p g n t -> p (g n t)"),
             )
 
+        def quantize_x_pass(c, g):
+            nc.vector.quantize_mx(
+                out=x_codes[c][:, g, :].bitcast(FP8X4),
+                scales=x_scales[c][:, g, :],
+                in_=x_grouped[c][:, g, :, :].rearrange("p n t -> p (n t)"),
+            )
+
         def turn_w(i):
             w_turned[i] = psum.tile([P, PASSES, 2, P], F32, name="wturned%d" % i, tag="bank")
             words = w_raw[i][:].bitcast(F32)
@@ -133,9 +144,10 @@ def tile_selfattention_pa_kernel(tc, x_bytes, x_scale, Wq, Wk, Wv, out_0, out_1,
                 in_=w_grouped[:, i0:i1, :].rearrange("p i n -> p (i n)"),
             )
 
-        def multiply(c, i):
-            acc[c, i] = psum.tile([P, CHUNK], F32, name="acc%d%d" % (c, i), tag="bank")
-            for g in range(PASSES):
+        def multiply(c, i, passes=(0, 1)):
+            if 0 in passes:
+                acc[c, i] = psum.tile([P, CHUNK], F32, name="acc%d%d" % (c, i), tag="bank")
+            for g in passes:
                 rows = slice(g * P, (g + 1) * P)
                 nc.tensor.matmul_mx(
                     out=acc[c, i][:],
@@ -155,42 +167,28 @@ def tile_selfattention_pa_kernel(tc, x_bytes, x_scale, Wq, Wk, Wv, out_0, out_1,
                 op=MAX,
             )
 
-        def pool_first(c):
-            for i in range(N_KV - LAG):
-                pool(c, i)
-            cols = slice(c * POOLED, (c + 1) * POOLED)
-            nc.sync.dma_start(out=k_out[:, cols], in_=kv_sb[c][:, 0, :])
-            nc.sync.dma_start(out=v_out[:, 0:N_KV - LAG - 1, cols], in_=kv_sb[c][:, 1:N_KV - LAG, :])
-
-        def pool_rest(c):
-            cols = slice(c * POOLED, (c + 1) * POOLED)
-            cut = N_KV - 1 if c == N_CHUNKS - 1 else N_KV
-            for i in range(N_KV - LAG, cut):
-                pool(c, i)
-            nc.sync.dma_start(out=v_out[:, N_KV - LAG - 1:cut - 1, cols], in_=kv_sb[c][:, N_KV - LAG:cut, :])
-            for i in range(cut, N_KV):
-                pool(c, i)
-                nc.sync.dma_start(out=v_out[:, i - 1:i, cols], in_=kv_sb[c][:, i:i + 1, :])
-
         def by_place(c, i):
             return acc[c, i][:].rearrange("p (w j) -> p j w", j=WINDOW)
 
-        def copy_late_halves(c):
-            for i in range(N_KV - LAG, N_KV):
-                nc.scalar.copy(out=late_half[:, i - (N_KV - LAG), :, :], in_=by_place(c, i)[:, 2:4, :])
+        def copy_half(c, i):
+            nc.scalar.copy(out=late_half[c, i][:], in_=by_place(c, i)[:, 2:4, :])
 
-        def pool_rest_shared(c):
-            for i in range(N_KV - LAG, N_KV):
-                k = i - (N_KV - LAG)
-                nc.vector.tensor_tensor(out=late_max[:, k, :, :], in0=by_place(c, i)[:, 0:2, :], in1=late_half[:, k, :, :], op=MAX)
-            nc.vector.tensor_tensor(
-                out=kv_sb[c][:, N_KV - LAG:N_KV, :], in0=late_max[:, :, 0, :], in1=late_max[:, :, 1, :], op=MAX
-            )
-            cols = slice(c * POOLED, (c + 1) * POOLED)
-            nc.sync.dma_start(out=v_out[:, N_KV - LAG - 1:N_KV - 1, cols], in_=kv_sb[c][:, N_KV - LAG:N_KV, :])
+        def max_half(c, i):
+            nc.vector.tensor_tensor(out=late_max[c][:, i, :, :], in0=by_place(c, i)[:, 0:2, :], in1=late_half[c, i][:], op=MAX)
 
-        def project_q(c):
+        def max_end(c, i0, i1):
+            nc.vector.tensor_tensor(out=kv_sb[c][:, i0:i1, :], in0=late_max[c][:, i0:i1, 0, :], in1=late_max[c][:, i0:i1, 1, :], op=MAX)
+
+        def store_k(c):
+            nc.sync.dma_start(out=k_out[:, c * POOLED:(c + 1) * POOLED], in_=kv_sb[c][:, 0, :])
+
+        def store_v(c, i0, i1):
+            nc.sync.dma_start(out=v_out[:, i0 - 1:i1 - 1, c * POOLED:(c + 1) * POOLED], in_=kv_sb[c][:, i0:i1, :])
+
+        def multiply_q(c):
             multiply(c, Q_TILE)
+
+        def finish_q(c):
             nc.scalar.copy(out=q_sb[c][:], in_=acc[c, Q_TILE][:])
             nc.sync.dma_start(out=q_out[:, c * CHUNK:(c + 1) * CHUNK], in_=q_sb[c][:])
 
@@ -198,74 +196,103 @@ def tile_selfattention_pa_kernel(tc, x_bytes, x_scale, Wq, Wk, Wv, out_0, out_1,
             nc.scalar.dma_start(out=scale[:], in_=scale_rows)
             load_x(0, 0)
             load_x(0, 1)
+            load_x(1, 0)
+            load_x(1, 1)
             for i in (0, 1, 2):
                 load_w(i)
-            load_x(1, 1)
+            load_x(2, 0)
             for i in (3, 4):
                 load_w(i)
-            load_x(1, 0)
-            for c in (2, 3):
-                load_x(c, 1)
-                load_x(c, 0)
-            load_w(Q_TILE)
+            load_x(2, 1)
+            load_w(5)
+            load_x(3, 1)
+            load_x(3, 0)
             nc.scalar.activation(out=warm[:, 1:2], in_=warm[:, 0:1], func=COPY, scale=1.0)
-
-            for g in range(PASSES):
-                widen(nc.scalar, 0, g, (0, 1))
-                widen(nc.vector, 0, g, (2, 3))
-            interleave(nc.vector, 0, 0, 0, halves=2)
-            interleave(nc.scalar, 0, 1, 0)
-            interleave(nc.vector, 0, 1, 1)
-            for i in (0, 1):
+            widen(nc.scalar, 0, 0, (0,))
+            widen(nc.vector, 0, 0, (1, 2, 3))
+            widen(nc.scalar, 0, 1, (0, 1))
+            widen(nc.vector, 0, 1, (2, 3))
+            interleave(nc.scalar, 0, 0, 0)
+            interleave(nc.vector, 0, 0, 1)
+            widen(nc.scalar, 1, 0, (0,))
+            widen(nc.vector, 1, 0, (1, 2, 3))
+            interleave(nc.scalar, 0, 1, 0, halves=2)
+            widen(nc.vector, 1, 1, ALL_PLANES)
+            interleave(nc.vector, 1, 0, 0, halves=2)
+            interleave(nc.vector, 1, 1, 0, halves=2)
+            for i in range(5):
                 turn_w(i)
                 copy_w(i)
+            widen(nc.vector, 2, 0, (0, 1))
+            quantize_w(0, 1)
             quantize_x(0)
-            quantize_w(0, 2)
-            widen(nc.vector, 1, 1, (0, 1))
-            for i in (2, 3, 4):
-                turn_w(i)
-                copy_w(i)
-            quantize_w(2, 4)
-            quantize_w(4, 5)
-            widen(nc.vector, 1, 1, (2, 3))
-            interleave(nc.gpsimd, 1, 1, 0)
-            for i in range(N_KV):
+            multiply(0, 0)
+            turn_w(5)
+            quantize_w(1, 3)
+            quantize_w(3, 5)
+            quantize_x(1)
+            widen(nc.scalar, 2, 1, (0, 1, 2))
+            widen(nc.scalar, 2, 0, (2, 3))
+            widen(nc.vector, 2, 1, (3,))
+            interleave(nc.gpsimd, 2, 1, 0, halves=2)
+            interleave(nc.gpsimd, 2, 0, 1)
+            interleave(nc.scalar, 2, 0, 0)
+            copy_w(5)
+            for i in range(1, 5):
                 multiply(0, i)
-            pool_first(0)
-            widen(nc.scalar, 1, 0, ALL_PLANES)
-            interleave(nc.scalar, 1, 0, 0)
-            turn_w(Q_TILE)
-            copy_w(Q_TILE)
-
-            for c in range(1, N_CHUNKS):
-                nxt = c + 1
-                if c == 1:
-                    interleave(nc.vector, c, 1, 1)
-                if c < N_CHUNKS - 1:
-                    interleave(nc.vector, c, 0, 1)
-                if nxt < N_CHUNKS:
-                    widen(nc.vector, nxt, 1, (2,) if nxt == N_CHUNKS - 1 else (1, 2))
-                quantize_x(c)
-                if c == N_CHUNKS - 2:
-                    quantize_w(Q_TILE, ROW_TILES)
-                if nxt < N_CHUNKS:
-                    widen(nc.scalar, nxt, 1, (0, 1) if nxt == N_CHUNKS - 1 else (0,))
-                    widen(nc.vector, nxt, 1, (3,))
-                    interleave(nc.gpsimd, nxt, 1, 0, halves=2)
-                if c == N_CHUNKS - 1:
-                    pool_rest_shared(c - 1)
-                else:
-                    pool_rest(c - 1)
-                for i in range(N_KV):
-                    if c == N_CHUNKS - 1 and i == Q_AFTER:
-                        project_q(c)
-                    multiply(c, i)
-                pool_first(c)
-                if nxt < N_CHUNKS:
-                    widen(nc.scalar, nxt, 0, ALL_PLANES)
-                    interleave(nc.scalar, nxt, 0, 0, halves=2 if nxt == N_CHUNKS - 1 else 1)
-                if c == N_CHUNKS - 2:
-                    copy_late_halves(c)
-                    for done in range(N_CHUNKS - 1):
-                        project_q(done)
-            pool_rest(N_CHUNKS - 1)
+            for i in range(5):
+                pool(0, i)
+            store_k(0)
+            store_v(0, 1, 5)
+            for i in range(5):
+                multiply(1, i)
+            pool(1, 0)
+            pool(1, 1)
+            widen(nc.scalar, 3, 1, (0, 1, 2))
+            widen(nc.scalar, 3, 0, ALL_PLANES)
+            quantize_w(5, 6)
+            multiply_q(0)
+            multiply_q(1)
+            quantize_x(2)
+            widen(nc.vector, 3, 1, (3,))
+            interleave(nc.gpsimd, 3, 1, 0, halves=2)
+            interleave(nc.scalar, 3, 0, 0, halves=2)
+            finish_q(0)
+            for i in (2, 3, 4):
+                pool(1, i)
+            store_k(1)
+            store_v(1, 1, 5)
+            for i in range(5):
+                multiply(2, i)
+            pool(2, 0)
+            pool(2, 1)
+            store_k(2)
+            store_v(2, 1, 2)
+            finish_q(1)
+            for i in (2, 3, 4):
+                copy_half(2, i)
+            multiply_q(2)
+            finish_q(2)
+            quantize_x(3)
+            for i in (2, 3, 4):
+                max_half(2, i)
+            max_end(2, 2, 5)
+            store_v(2, 2, 5)
+            for i in (0, 1, 2):
+                multiply(3, i)
+            copy_half(3, 0)
+            copy_half(3, 1)
+            multiply_q(3)
+            for i in (3, 4):
+                multiply(3, i)
+            finish_q(3)
+            max_half(3, 0)
+            max_half(3, 1)
+            pool(3, 2)
+            max_end(3, 0, 2)
+            store_k(3)
+            store_v(3, 1, 3)
+            pool(3, 3)
+            store_v(3, 3, 4)
+            pool(3, 4)
+            store_v(3, 4, 5)

@@ -82,6 +82,9 @@ def tile_selfattention_pa_kernel(tc, x_bytes, x_scale, Wq, Wk, Wv, out_0, out_1,
         def load_x(c, g):
             nc.sync.dma_start(out=x_raw[c, g][:], in_=x_rows[g][:, :, c * CHUNK:(c + 1) * CHUNK])
 
+        def load_x_planes(c, g, t0, t1):
+            nc.sync.dma_start(out=x_raw[c, g][:, t0:t1, :], in_=x_rows[g][:, t0:t1, c * CHUNK:(c + 1) * CHUNK])
+
         def load_w(i):
             nc.sync.dma_start(out=w_raw[i][:], in_=w_rows[i])
 
@@ -194,8 +197,10 @@ def tile_selfattention_pa_kernel(tc, x_bytes, x_scale, Wq, Wk, Wv, out_0, out_1,
 
         with tc.manual_schedule():
             nc.scalar.dma_start(out=scale[:], in_=scale_rows)
-            load_x(0, 0)
-            load_x(0, 1)
+            load_x_planes(0, 0, 0, 2)
+            load_x_planes(0, 0, 2, 4)
+            load_x_planes(0, 1, 0, 2)
+            load_x_planes(0, 1, 2, 4)
             load_x(1, 0)
             load_x(1, 1)
             for i in (0, 1, 2):
@@ -210,8 +215,8 @@ def tile_selfattention_pa_kernel(tc, x_bytes, x_scale, Wq, Wk, Wv, out_0, out_1,
             nc.scalar.activation(out=warm[:, 1:2], in_=warm[:, 0:1], func=COPY, scale=1.0)
             widen(nc.scalar, 0, 0, (0,))
             widen(nc.vector, 0, 0, (1, 2, 3))
-            widen(nc.scalar, 0, 1, (0, 1))
-            widen(nc.vector, 0, 1, (2, 3))
+            widen(nc.scalar, 0, 1, (0, 2))
+            widen(nc.vector, 0, 1, (1, 3))
             interleave(nc.scalar, 0, 0, 0)
             interleave(nc.vector, 0, 0, 1)
             widen(nc.scalar, 1, 0, (0,))
@@ -236,8 +241,8 @@ def tile_selfattention_pa_kernel(tc, x_bytes, x_scale, Wq, Wk, Wv, out_0, out_1,
             widen(nc.vector, 2, 1, (3,))
             interleave(nc.gpsimd, 2, 1, 0, halves=2)
             interleave(nc.gpsimd, 2, 0, 1)
-            interleave(nc.scalar, 2, 0, 0)
             copy_w(5)
+            interleave(nc.scalar, 2, 0, 0)
             for i in range(1, 5):
                 multiply(0, i)
             for i in range(5):
@@ -273,26 +278,26 @@ def tile_selfattention_pa_kernel(tc, x_bytes, x_scale, Wq, Wk, Wv, out_0, out_1,
                 copy_half(2, i)
             multiply_q(2)
             finish_q(2)
-            quantize_x(3)
+            for g in range(PASSES):
+                quantize_x_pass(3, g)
+            for g in range(PASSES):
+                for i in (0, 1, 2):
+                    multiply(3, i, passes=(g,))
             for i in (2, 3, 4):
                 max_half(2, i)
+            multiply(3, 3)
+            multiply_q(3)
+            multiply(3, 4)
+            pool(3, 0)
+            store_k(3)
             max_end(2, 2, 5)
             store_v(2, 2, 5)
-            for i in (0, 1, 2):
-                multiply(3, i)
-            copy_half(3, 0)
-            copy_half(3, 1)
-            multiply_q(3)
-            for i in (3, 4):
-                multiply(3, i)
+            for i in (1, 2, 3):
+                copy_half(3, i)
             finish_q(3)
-            max_half(3, 0)
-            max_half(3, 1)
-            pool(3, 2)
-            max_end(3, 0, 2)
-            store_k(3)
-            store_v(3, 1, 3)
-            pool(3, 3)
-            store_v(3, 3, 4)
+            for i in (1, 2, 3):
+                max_half(3, i)
+            max_end(3, 1, 4)
+            store_v(3, 1, 4)
             pool(3, 4)
             store_v(3, 4, 5)

@@ -215,8 +215,8 @@ def tile_selfattention_pa_kernel(tc, x_bytes, x_scale, Wq, Wk, Wv, out_0, out_1,
             nc.scalar.activation(out=warm[:, 1:2], in_=warm[:, 0:1], func=COPY, scale=1.0)
             widen(nc.scalar, 0, 0, (0,))
             widen(nc.vector, 0, 0, (1, 2, 3))
-            widen(nc.scalar, 0, 1, (0, 2))
-            widen(nc.vector, 0, 1, (1, 3))
+            widen(nc.scalar, 0, 1, (0,))
+            widen(nc.vector, 0, 1, (1, 2, 3))
             interleave(nc.scalar, 0, 0, 0)
             interleave(nc.vector, 0, 0, 1)
             widen(nc.scalar, 1, 0, (0,))
@@ -228,7 +228,7 @@ def tile_selfattention_pa_kernel(tc, x_bytes, x_scale, Wq, Wk, Wv, out_0, out_1,
             for i in range(5):
                 turn_w(i)
                 copy_w(i)
-            widen(nc.vector, 2, 0, (0, 1))
+            widen(nc.vector, 2, 0, (0,))
             quantize_w(0, 1)
             quantize_x(0)
             multiply(0, 0)
@@ -237,7 +237,7 @@ def tile_selfattention_pa_kernel(tc, x_bytes, x_scale, Wq, Wk, Wv, out_0, out_1,
             quantize_w(3, 5)
             quantize_x(1)
             widen(nc.scalar, 2, 1, (0, 1, 2))
-            widen(nc.scalar, 2, 0, (2, 3))
+            widen(nc.scalar, 2, 0, (1, 2, 3))
             widen(nc.vector, 2, 1, (3,))
             interleave(nc.gpsimd, 2, 1, 0, halves=2)
             interleave(nc.gpsimd, 2, 0, 1)

@@ -262,7 +262,6 @@ def tile_selfattention_pa_kernel(tc, x_bytes, x_scale, Wq, Wk, Wv, out_0, out_1,
             widen(nc.vector, 3, 1, (3,))
             interleave(nc.gpsimd, 3, 1, 0, halves=2)
             interleave(nc.scalar, 3, 0, 0, halves=2)
-            finish_q(0)
             for i in (2, 3, 4):
                 pool(1, i)
             store_k(1)
@@ -273,6 +272,7 @@ def tile_selfattention_pa_kernel(tc, x_bytes, x_scale, Wq, Wk, Wv, out_0, out_1,
             pool(2, 1)
             store_k(2)
             store_v(2, 1, 2)
+            finish_q(0)
             finish_q(1)
             for i in (2, 3, 4):
                 copy_half(2, i)
@@ -297,7 +297,9 @@ def tile_selfattention_pa_kernel(tc, x_bytes, x_scale, Wq, Wk, Wv, out_0, out_1,
             finish_q(3)
             for i in (1, 2, 3):
                 max_half(3, i)
-            max_end(3, 1, 4)
-            store_v(3, 1, 4)
+            max_end(3, 1, 3)
+            store_v(3, 1, 3)
+            max_end(3, 3, 4)
+            store_v(3, 3, 4)
             pool(3, 4)
             store_v(3, 4, 5)

from contextlib import ExitStack

import concourse.mybir as mybir
from concourse.masks import make_identity

FLOPS = 2 * 768 * 1024 * 2048

F32 = mybir.dt.float32
BF16 = mybir.dt.bfloat16
U32 = mybir.dt.uint32
U8 = mybir.dt.uint8
FP8 = mybir.dt.float8_e4m3fn
FP8X4 = mybir.dt.float8_e4m3fn_x4
COPY = mybir.ActivationFunctionType.Copy
MULT = mybir.AluOpType.mult
ADD = mybir.AluOpType.add
MAX = mybir.AluOpType.max

P = 128
PACK = 4
PASSES = 2
K_PASS = P * PACK
CHUNK = 512
N_CHUNKS = 4
HALF = CHUNK // 2
WINDOW = 4
POOLED = CHUNK // WINDOW
ROW_TILES = 6
N_KV = ROW_TILES - 1
Q_TILE = ROW_TILES - 1
LAG = 3
Q_AFTER = 2
ALL_PLANES = (0, 1, 2, 3)


def tile_selfattention_pa_kernel(tc, x_bytes, x_scale, Wq, Wk, Wv, out_0, out_1, out_2):
    nc = tc.nc
    x_rows = x_bytes.flatten_outer_dims().rearrange("(g p t) n -> g p t n", p=P, t=PACK)
    scale_rows = x_scale.flatten_outer_dims().rearrange("(g p t) o -> p g (t o)", p=P, t=PACK)
    wv_rows = Wv.rearrange("(m p) k -> m p k", p=P)
    w_rows = [Wk] + [wv_rows[m] for m in range(4)] + [Wq]
    q_out = out_0.flatten_outer_dims()
    k_out = out_1.flatten_outer_dims()
    v_out = out_2.flatten_outer_dims().rearrange("(m p) w -> p m w", p=P)

    with ExitStack() as ctx:
        keep = ctx.enter_context(tc.tile_pool(name="keep", bufs=1))
        psum = ctx.enter_context(tc.psum_pool(name="psum", bufs=8))

        ident = keep.tile([P, P], F32, name="ident")
        make_identity(nc, ident[:])
        warm = keep.tile([P, 2], F32, name="warm")
        nc.vector.memset(warm[:], 0.0)

        scale = keep.tile([P, PASSES, PACK], F32, name="scale")
        x_raw = {}
        x_wide = {}
        for c in range(N_CHUNKS):
            for g in range(PASSES):
                x_raw[c, g] = keep.tile([P, PACK, CHUNK], U8, name="xraw%d%d" % (c, g))
                x_wide[c, g] = keep.tile([P, PACK, CHUNK], BF16, name="xwide%d%d" % (c, g))
        x_grouped = [
            keep.tile([P, PASSES, CHUNK, PACK], BF16, name="xgrouped%d" % c, align_bytes=64) for c in range(N_CHUNKS)
        ]
        x_codes = [keep.tile([P, PASSES, CHUNK], U32, name="xcodes%d" % c, align_bytes=64) for c in range(N_CHUNKS)]
        x_scales = [keep.tile([P, PASSES, CHUNK], U8, name="xscales%d" % c, align_bytes=64) for c in range(N_CHUNKS)]
        w_raw = [keep.tile([P, PASSES * K_PASS], BF16, name="wraw%d" % i) for i in range(ROW_TILES)]
        w_grouped = keep.tile([P, ROW_TILES, PASSES * K_PASS], BF16, name="wgrouped", align_bytes=64)
        w_codes = keep.tile([P, ROW_TILES, PASSES * P], U32, name="wcodes", align_bytes=64)
        w_scales = keep.tile([P, ROW_TILES, PASSES * P], U8, name="wscales", align_bytes=64)
        q_sb = [keep.tile([P, CHUNK], F32, name="qsb%d" % c) for c in range(N_CHUNKS)]
        kv_sb = [keep.tile([P, N_KV, POOLED], F32, name="kvsb%d" % c) for c in range(N_CHUNKS)]
        late_half = {}
        late_max = {}
        for c in (2, 3):
            late_max[c] = keep.tile([P, N_KV, 2, POOLED], F32, name="latemax%d" % c)
            for i in range(N_KV):
                late_half[c, i] = keep.tile([P, 2, POOLED], F32, name="latehalf%d%d" % (c, i))
        w_turned = {}
        acc = {}

        def load_x(c, g):
            nc.sync.dma_start(out=x_raw[c, g][:], in_=x_rows[g][:, :, c * CHUNK:(c + 1) * CHUNK])

        def load_x_planes(c, g, t0, t1):
            nc.sync.dma_start(out=x_raw[c, g][:, t0:t1, :], in_=x_rows[g][:, t0:t1, c * CHUNK:(c + 1) * CHUNK])

        def load_w(i):
            nc.sync.dma_start(out=w_raw[i][:], in_=w_rows[i])

        def widen(engine, c, g, planes):
            for t in planes:
                src = x_raw[c, g][:, t, :].bitcast(FP8)
                dst = x_wide[c, g][:, t, :]
                if engine is nc.scalar:
                    nc.scalar.activation(out=dst, in_=src, func=COPY, scale=scale[:, g, t:t + 1])
                else:
                    nc.vector.tensor_scalar(out=dst, in0=src, scalar1=scale[:, g, t:t + 1], scalar2=None, op0=MULT)

        def interleave(engine, c, g, h, halves=1):
            cols = slice(h * HALF, (h + halves) * HALF)
            src = x_wide[c, g][:, :, cols]
            dst = x_grouped[c][:, g, cols, :]
            if engine is nc.gpsimd:
                nc.gpsimd.tensor_scalar(
                    out=dst, in0=src.rearrange("p t n -> p n t"), scalar1=1.0, scalar2=0.0, op0=MULT, op1=ADD
                )
            else:
                src_runs = src.rearrange("p t (b i) -> p b t i", i=4)
                dst_runs = dst.rearrange("p (b i) t -> p b t i", i=4)
                if engine is nc.scalar:
                    nc.scalar.copy(out=dst_runs, in_=src_runs)
                else:
                    nc.vector.tensor_copy(out=dst_runs, in_=src_runs)

        def quantize_x(c):
            nc.vector.quantize_mx(
                out=x_codes[c][:].rearrange("p g n -> p (g n)").bitcast(FP8X4),
                scales=x_scales[c][:].rearrange("p g n -> p (g n)"),
                in_=x_grouped[c][:].rearrange("p g n t -> p (g n t)"),
            )

        def quantize_x_pass(c, g):
            nc.vector.quantize_mx(
                out=x_codes[c][:, g, :].bitcast(FP8X4),
                scales=x_scales[c][:, g, :],
                in_=x_grouped[c][:, g, :, :].rearrange("p n t -> p (n t)"),
            )

        def turn_w(i):
            w_turned[i] = psum.tile([P, PASSES, 2, P], F32, name="wturned%d" % i, tag="bank")
            words = w_raw[i][:].bitcast(F32)
            for g in range(PASSES):
                for u in range(2):
                    nc.tensor.transpose(w_turned[i][:, g, u, :], words[:, 256 * g + u:256 * (g + 1):2], ident[:])

        def copy_w(i):
            nc.scalar.copy(
                out=w_grouped[:, i, :].bitcast(F32).rearrange("p (g r u) -> p g r u", g=PASSES, u=2),
                in_=w_turned[i][:].rearrange("p g u r -> p g r u"),
            )

        def quantize_w(i0, i1):
            nc.vector.quantize_mx(
                out=w_codes[:, i0:i1, :].rearrange("p i n -> p (i n)").bitcast(FP8X4),
                scales=w_scales[:, i0:i1, :].rearrange("p i n -> p (i n)"),
                in_=w_grouped[:, i0:i1, :].rearrange("p i n -> p (i n)"),
            )

        def multiply(c, i, passes=(0, 1)):
            if 0 in passes:
                acc[c, i] = psum.tile([P, CHUNK], F32, name="acc%d%d" % (c, i), tag="bank")
            for g in passes:
                rows = slice(g * P, (g + 1) * P)
                nc.tensor.matmul_mx(
                    out=acc[c, i][:],
                    lhsT=w_codes[:, i, rows].bitcast(FP8X4),
                    lhsT_scale=w_scales[:, i, rows],
                    rhs=x_codes[c][:, g, :].bitcast(FP8X4),
                    rhs_scale=x_scales[c][:, g, :],
                    start=(g == 0),
                    stop=(g == PASSES - 1),
                )

        def pool(c, i):
            nc.vector.tensor_reduce(
                out=kv_sb[c][:, i, :],
                in_=acc[c, i][:].rearrange("p (w j) -> p w j", j=WINDOW),
                axis=mybir.AxisListType.X,
                op=MAX,
            )

        def by_place(c, i):
            return acc[c, i][:].rearrange("p (w j) -> p j w", j=WINDOW)

        def copy_half(c, i):
            nc.scalar.copy(out=late_half[c, i][:], in_=by_place(c, i)[:, 2:4, :])

        def max_half(c, i):
            nc.vector.tensor_tensor(out=late_max[c][:, i, :, :], in0=by_place(c, i)[:, 0:2, :], in1=late_half[c, i][:], op=MAX)

        def max_end(c, i0, i1):
            nc.vector.tensor_tensor(out=kv_sb[c][:, i0:i1, :], in0=late_max[c][:, i0:i1, 0, :], in1=late_max[c][:, i0:i1, 1, :], op=MAX)

        def store_k(c):
            nc.sync.dma_start(out=k_out[:, c * POOLED:(c + 1) * POOLED], in_=kv_sb[c][:, 0, :])

        def store_v(c, i0, i1):
            nc.sync.dma_start(out=v_out[:, i0 - 1:i1 - 1, c * POOLED:(c + 1) * POOLED], in_=kv_sb[c][:, i0:i1, :])

        def multiply_q(c):
            multiply(c, Q_TILE)

        def finish_q(c):
            nc.scalar.copy(out=q_sb[c][:], in_=acc[c, Q_TILE][:])
            nc.sync.dma_start(out=q_out[:, c * CHUNK:(c + 1) * CHUNK], in_=q_sb[c][:])

        with tc.manual_schedule():
            nc.scalar.dma_start(out=scale[:], in_=scale_rows)
            load_x_planes(0, 0, 0, 2)
            load_x_planes(0, 0, 2, 4)
            load_x_planes(0, 1, 0, 2)
            load_x_planes(0, 1, 2, 4)
            load_x(1, 0)
            load_x(1, 1)
            for i in (0, 1, 2):
                load_w(i)
            load_x(2, 0)
            for i in (3, 4):
                load_w(i)
            load_x(2, 1)
            load_w(5)
            load_x(3, 1)
            load_x(3, 0)
            nc.scalar.activation(out=warm[:, 1:2], in_=warm[:, 0:1], func=COPY, scale=1.0)
            widen(nc.scalar, 0, 0, (0,))
            widen(nc.vector, 0, 0, (1, 2, 3))
            widen(nc.scalar, 0, 1, (0,))
            widen(nc.vector, 0, 1, (1, 2, 3))
            interleave(nc.scalar, 0, 0, 0)
            interleave(nc.vector, 0, 0, 1)
            widen(nc.scalar, 1, 0, (0,))
            widen(nc.vector, 1, 0, (1, 2, 3))
            interleave(nc.scalar, 0, 1, 0, halves=2)
            widen(nc.vector, 1, 1, ALL_PLANES)
            interleave(nc.vector, 1, 0, 0, halves=2)
            interleave(nc.vector, 1, 1, 0, halves=2)
            for i in range(5):
                turn_w(i)
                copy_w(i)
            widen(nc.vector, 2, 0, (0,))
            quantize_w(0, 1)
            quantize_x(0)
            multiply(0, 0)
            turn_w(5)
            quantize_w(1, 3)
            quantize_w(3, 5)
            quantize_x(1)
            widen(nc.scalar, 2, 1, (0, 1, 2))
            widen(nc.scalar, 2, 0, (1, 2, 3))
            widen(nc.vector, 2, 1, (3,))
            interleave(nc.gpsimd, 2, 1, 0, halves=2)
            interleave(nc.gpsimd, 2, 0, 1)
            copy_w(5)
            interleave(nc.scalar, 2, 0, 0)
            for i in range(1, 5):
                multiply(0, i)
            for i in range(5):
                pool(0, i)
            store_k(0)
            store_v(0, 1, 5)
            for i in range(5):
                multiply(1, i)
            pool(1, 0)
            pool(1, 1)
            widen(nc.scalar, 3, 1, (0, 1, 2))
            widen(nc.scalar, 3, 0, ALL_PLANES)
            quantize_w(5, 6)
            multiply_q(0)
            multiply_q(1)
            quantize_x(2)
            widen(nc.vector, 3, 1, (3,))
            interleave(nc.gpsimd, 3, 1, 0, halves=2)
            interleave(nc.scalar, 3, 0, 0, halves=2)
            for i in (2, 3, 4):
                pool(1, i)
            store_k(1)
            store_v(1, 1, 5)
            for i in range(5):
                multiply(2, i)
            pool(2, 0)
            pool(2, 1)
            store_k(2)
            store_v(2, 1, 2)
            finish_q(0)
            finish_q(1)
            for i in (2, 3, 4):
                copy_half(2, i)
            multiply_q(2)
            finish_q(2)
            for g in range(PASSES):
                quantize_x_pass(3, g)
            for g in range(PASSES):
                for i in (0, 1, 2):
                    multiply(3, i, passes=(g,))
            for i in (2, 3, 4):
                max_half(2, i)
            multiply(3, 3)
            multiply_q(3)
            multiply(3, 4)
            pool(3, 0)
            store_k(3)
            max_end(2, 2, 5)
            store_v(2, 2, 5)
            for i in (1, 2, 3):
                copy_half(3, i)
            finish_q(3)
            for i in (1, 2, 3):
                max_half(3, i)
            max_end(3, 1, 3)
            store_v(3, 1, 3)
            max_end(3, 3, 4)
            store_v(3, 3, 4)
            pool(3, 4)
            store_v(3, 4, 5)
